import numpy as np
import ml_dtypes


def mxq(x, axis, fmt="e4m3"):
    dtype, down = {"e4m3": (ml_dtypes.float8_e4m3fn, 7), "e5m2": (ml_dtypes.float8_e5m2, 14)}[fmt]
    v = np.moveaxis(np.asarray(x, np.float32).astype(ml_dtypes.bfloat16).astype(np.float64), axis, -1)
    blocks = v.reshape(v.shape[:-1] + (-1, 32))
    amax = np.abs(blocks).max(-1, keepdims=True)
    byte = np.maximum(np.where(amax > 0, np.frexp(amax)[1] - 1 + 127, 0) - down, 1)
    scale = np.exp2(byte - 127.0)
    codes = (blocks / scale).astype(np.float32).astype(dtype).astype(np.float64)
    return np.moveaxis((codes * scale).reshape(v.shape), -1, axis)


WIDE = False


def mx_kscale(k):
    if not WIDE:
        return np.ones(k)
    levels = np.array([10, -10, 5, -5, 0])
    a = np.random.permutation(np.resize(levels, k // 512 * 4)).reshape(k // 512, 4)
    idx = np.arange(k)
    return np.exp2(a[idx // 512, idx % 128 // 32])


BF16 = ml_dtypes.bfloat16


def bf(x):
    return np.asarray(x, np.float32).astype(BF16)


def f64(x):
    return np.asarray(x).astype(np.float64)


B, I, H = 256, 2048, 2048
C = I + H


def sigmoid(v):
    return 1.0 / (1.0 + np.exp(-v))


def setup_inputs():
    s, t = mx_kscale(I), mx_kscale(H)
    d = np.concatenate([s, t])[:, None]
    return {"x": bf(np.random.standard_normal((B, I)) * s),
            "h_prev": bf(np.random.standard_normal((B, H)) * t),
            "W_r": bf(np.random.standard_normal((C, H)) / np.sqrt(C) / d),
            "b_r": bf(np.random.standard_normal(H) * 0.5),
            "W_n": bf(np.random.standard_normal((C, H)) / np.sqrt(C) / d),
            "b_n": bf(np.random.standard_normal(H) * 0.5)}


def reference(x, h_prev, W_r, b_r, W_n, b_n):
    x, h_prev, W_r, W_n = f64(x), f64(h_prev), f64(W_r), f64(W_n)
    xq = mxq(x, 1, "e4m3")
    hq = mxq(h_prev, 1, "e4m3")
    r = sigmoid((xq @ mxq(W_r[:I], 0, "e4m3")) + (hq @ mxq(W_r[I:], 0, "e4m3")) + f64(b_r))
    n = np.tanh((xq @ mxq(W_n[:I], 0, "e4m3")) + (mxq(r * h_prev, 1, "e4m3") @ mxq(W_n[I:], 0, "e4m3")) + f64(b_n))
    return n

@@ -1,0 +1,284 @@
+from contextlib import ExitStack
+
+import concourse.mybir as mybir
+from concourse.masks import make_identity
+
+FLOPS = 2 * 256 * 2048 * 2048 * 4
+
+BF16 = mybir.dt.bfloat16
+F32 = mybir.dt.float32
+U32 = mybir.dt.uint32
+U8 = mybir.dt.uint8
+FP8X4 = mybir.dt.float8_e4m3fn_x4
+ACT = mybir.ActivationFunctionType
+ALU = mybir.AluOpType
+
+P = 128
+B = 256
+H = 2048
+MANUAL = True
+RAW_BUFS = 5
+CV = 480
+CV_LAST = 192
+SIG_A = 16
+SIG_B = 22
+
+
+def tile_grucell_pa_kernel(tc, x, h_prev, W_r, b_r, W_n, b_n, out):
+    nc = tc.nc
+    with ExitStack() as ctx:
+        const = ctx.enter_context(tc.tile_pool(name="const", bufs=1))
+        rawp = ctx.enter_context(tc.tile_pool(name="rawp", bufs=RAW_BUFS))
+        grpp = ctx.enter_context(tc.tile_pool(name="grpp", bufs=4))
+        codp = ctx.enter_context(tc.tile_pool(name="codp", bufs=1))
+        gate = ctx.enter_context(tc.tile_pool(name="gate", bufs=1))
+        epi = ctx.enter_context(tc.tile_pool(name="epi", bufs=4))
+        psum = ctx.enter_context(tc.psum_pool(name="psum", bufs=1))
+
+        ident_bf = const.tile([P, P], BF16, name="ident_bf")
+        ident_f = const.tile([P, P], F32, name="ident_f")
+        make_identity(nc, ident_bf[:])
+        make_identity(nc, ident_f[:])
+        brt = const.tile([P, P], BF16, name="brt")
+        br = const.tile([P, 16], F32, name="br")
+        bias_n = const.tile([P, H], BF16, name="bias_n")
+        hg = const.tile([P, 4096], BF16, name="hg", align_bytes=64)
+        act_codes = {}
+        act_planes = {}
+        for nm in ("x", "h", "rh"):
+            act_codes[nm] = const.tile([P, 1024], U32, name="codes_" + nm, align_bytes=64)
+            act_planes[nm] = const.tile([P, 1024], U8, name="plane_" + nm, align_bytes=64)
+
+        if MANUAL:
+            ctx.enter_context(tc.manual_schedule())
+
+        raw = {}
+        state = {"next_load": 1}
+
+        def chunk_rows(k):
+            w = W_r if k < 8 else W_n
+            c = k % 8
+            return w[512 * c:512 * c + 512, :], c
+
+        def emit_load(k):
+            t = rawp.tile([P, 8192], BF16, name="raw%d" % k, tag="raw")
+            raw[k] = t
+            rows, c = chunk_rows(k)
+            if c < 4:
+                nc.sync.dma_start(out=t[:], in_=rows.rearrange("(p j) n -> p (j n)", j=4))
+            else:
+                nc.sync.dma_start(out=t[:].rearrange("p (t n) -> p t n", t=4),
+                                  in_=rows.rearrange("(t p) n -> p t n", p=P))
+            if k == 9:
+                nc.sync.dma_start(out=bias_n[:], in_=b_n.partition_broadcast(P))
+
+        def next_load():
+            k = state["next_load"]
+            if k < 16:
+                emit_load(k)
+                state["next_load"] = k + 1
+
+        nc.vector.memset(brt[:], 0.0)
+        raw[0] = rawp.tile([P, 8192], BF16, name="raw0", tag="raw")
+        xh = rawp.tile([P, 8192], BF16, name="xh", tag="raw")
+        raw0v = raw[0][:].rearrange("p (t n) -> p t n", t=4)
+        w0 = W_r[0:512, :].rearrange("(p j) n -> p j n", j=4)
+        for q in (0, 1):
+            nc.sync.dma_start(out=raw0v[:, :, 512 * q:512 * q + 512], in_=w0[:, :, 512 * q:512 * q + 512])
+        for a in (0, 1):
+            nc.sync.dma_start(out=xh[:, 4096 + 2048 * a:4096 + 2048 * a + 2048], in_=h_prev[P * a:P * a + P, :])
+        for a in (0, 1):
+            nc.sync.dma_start(out=xh[:, 2048 * a:2048 * a + 2048], in_=x[P * a:P * a + P, :])
+        for q in (2, 3):
+            nc.sync.dma_start(out=raw0v[:, :, 512 * q:512 * q + 512], in_=w0[:, :, 512 * q:512 * q + 512])
+        nc.sync.dma_start(out=brt[0:16, :], in_=b_r.rearrange("(i p) -> i p", p=P))
+        for k in range(RAW_BUFS - 2):
+            next_load()
+
+        units = []
+        for c in range(8):
+            units.append((c, 0, 1024, CV, c % 4))
+            units.append((c, 1024, 1024, CV, 4 + c))
+        for j in range(14):
+            units.append((8 + j // 2, 1024 * (j % 2), 1024, CV, j % 12))
+        for j in range(4):
+            units.append((15, 512 * j, 512, CV_LAST, 2 + j))
+        last_use = {}
+        for s, u in enumerate(units):
+            last_use[u[0]] = s
+
+        grouped = {}
+        codes = {}
+        planes = {}
+
+        def regroup(s):
+            k, n0, w, cv, slot = units[s]
+            g = grpp.tile([P, 4096], BF16, name="grp%d" % s, tag="grp", align_bytes=64)
+            grouped[s] = g
+            src = raw[k][:].rearrange("p (t n) -> p t n", t=4)
+            dst = g[:, 0:4 * w].rearrange("p (n t) -> p n t", t=4)
+            nc.vector.tensor_copy(
+                out=dst[:, 0:cv, :].rearrange("p (c i) t -> p c t i", i=4),
+                in_=src[:, :, n0:n0 + cv].rearrange("p t (c i) -> p c t i", i=4))
+            nc.scalar.copy(
+                out=dst[:, cv:w, :].rearrange("p (c i) t -> p c t i", i=4),
+                in_=src[:, :, n0 + cv:n0 + w].rearrange("p t (c i) -> p c t i", i=4))
+            if last_use[k] == s:
+                next_load()
+
+        def quantise(s):
+            k, n0, w, cv, slot = units[s]
+            cw = codp.tile([P, 1024], U32, name="cw%d" % s, tag="cw%d" % slot, align_bytes=64)
+            cs = codp.tile([P, 1024], U8, name="cs%d" % s, tag="cs%d" % slot, align_bytes=64)
+            codes[s] = cw
+            planes[s] = cs
+            nc.vector.quantize_mx(out=cw[:, 0:w].bitcast(FP8X4), scales=cs[:, 0:w], in_=grouped[s][:, 0:4 * w])
+
+        racc = {}
+
+        def mm_r(s):
+            k, n0, w, cv, slot = units[s]
+            half = n0 // 1024
+            nm = "x" if k < 4 else "h"
+            a0 = 256 * (k % 4)
+            for i in range(8):
+                nc.tensor.matmul_mx(
+                    out=racc[i][:, 256 * half:256 * half + 256],
+                    lhsT=codes[s][:, P * i:P * i + P].bitcast(FP8X4),
+                    lhsT_scale=planes[s][:, P * i:P * i + P],
+                    rhs=act_codes[nm][:, a0:a0 + 256].bitcast(FP8X4),
+                    rhs_scale=act_planes[nm][:, a0:a0 + 256],
+                    start=(k == 0), stop=(k == 7))
+
+        nacc = {}
+
+        def mm_n(s):
+            k, n0, w, cv, slot = units[s]
+            c = k - 8
+            nm = "x" if c < 4 else "rh"
+            for j in range(w // 512):
+                nb = n0 // 512 + j
+                for a in range(2):
+                    a0 = 256 * (c % 4) + P * a
+                    nc.tensor.matmul_mx(
+                        out=nacc[(a, nb)][:],
+                        lhsT=act_codes[nm][:, a0:a0 + P].bitcast(FP8X4),
+                        lhsT_scale=act_planes[nm][:, a0:a0 + P],
+                        rhs=codes[s][:, 512 * j:512 * j + 512].bitcast(FP8X4),
+                        rhs_scale=planes[s][:, 512 * j:512 * j + 512],
+                        start=(c == 0), stop=(c == 7))
+
+        r_sb = {}
+
+        def sigmoids(half):
+            r = gate.tile([P, 8, 256], F32, name="r_sb%d" % half, tag="r_sb")
+            r_sb[half] = r
+            for i in range(8):
+                nc.scalar.activation(out=r[:, i, :], in_=racc[i][:, 256 * half:256 * half + 256],
+                                     func=ACT.Sigmoid, bias=br[:, 8 * half + i:8 * half + i + 1], scale=1.0)
+
+        def gate_h(half):
+            rhg = gate.tile([P, 2048], BF16, name="rhg%d" % half, tag="rhg", align_bytes=64)
+            nc.vector.tensor_tensor(
+                out=rhg[:].rearrange("p (g b t) -> p g b t", g=2, t=4),
+                in0=r_sb[half][:].rearrange("p (g t) b -> p g b t", g=2),
+                in1=hg[:, 2048 * half:2048 * half + 2048].rearrange("p (g b t) -> p g b t", g=2, t=4),
+                op=ALU.mult)
+            return rhg
+
+        def quantise_rh(half, rhg):
+            nc.vector.quantize_mx(out=act_codes["rh"][:, 512 * half:512 * half + 512].bitcast(FP8X4),
+                                  scales=act_planes["rh"][:, 512 * half:512 * half + 512], in_=rhg[:])
+
+        def epilogue(nb):
+            for a in range(2):
+                pre = epi.tile([P, 512], F32, name="pre%d_%d" % (nb, a), tag="pre")
+                nc.vector.tensor_tensor(out=pre[:], in0=nacc[(a, nb)][:], in1=bias_n[:, 512 * nb:512 * nb + 512],
+                                        op=ALU.add)
+                res = epi.tile([P, 512], F32, name="res%d_%d" % (nb, a), tag="res")
+                nc.scalar.activation(out=res[:], in_=pre[:], func=ACT.Tanh)
+                nc.sync.dma_start(out=out[P * a:P * a + P, 512 * nb:512 * nb + 512], in_=res[:])
+
+        def transposes():
+            hts = []
+            for g in range(4):
+                ht = psum.tile([P, 4, 256], BF16, name="ht%d" % g, tag="bank%d" % g)
+                hts.append(ht)
+                for t in range(4):
+                    for a in range(2):
+                        c0 = 4096 + 2048 * a + 512 * g + P * t
+                        nc.tensor.transpose(ht[:, t, P * a:P * a + P], xh[:, c0:c0 + P], ident_bf[:])
+            xw = xh[:, 0:4096].bitcast(F32)
+            xts = []
+            for g in range(4):
+                xt = psum.tile([P, 2, 256], F32, name="xt%d" % g, tag="bank%d" % (4 + g))
+                xts.append(xt)
+                for u in range(2):
+                    for a in range(2):
+                        c0 = 1024 * a + 256 * g + u
+                        nc.tensor.transpose(xt[:, u, P * a:P * a + P], xw[:, c0:c0 + 255:2], ident_f[:])
+            return hts, xts
+
+        regroup(0)
+        hts, xts = transposes()
+        next_load()
+        quantise(0)
+        for g in range(4):
+            nc.scalar.copy(out=hg[:, 1024 * g:1024 * g + 1024].rearrange("p (b t) -> p b t", t=4),
+                           in_=hts[g][:].rearrange("p t b -> p b t"))
+        regroup(1)
+        nc.vector.quantize_mx(out=act_codes["h"][:].bitcast(FP8X4), scales=act_planes["h"][:], in_=hg[:])
+        xg = grpp.tile([P, 4096], BF16, name="xg", tag="grp", align_bytes=64)
+        xgw = xg[:].bitcast(F32)
+        for g in range(4):
+            nc.vector.tensor_copy(out=xgw[:, 512 * g:512 * g + 512].rearrange("p (b u) -> p b u", u=2),
+                                  in_=xts[g][:].rearrange("p u b -> p b u"))
+        nc.vector.quantize_mx(out=act_codes["x"][:].bitcast(FP8X4), scales=act_planes["x"][:], in_=xg[:])
+        brp = psum.tile([P, P], BF16, name="brp", tag="bank0")
+        nc.tensor.transpose(brp[:], brt[:], ident_bf[:])
+        nc.vector.tensor_copy(out=br[:], in_=brp[:, 0:16])
+        for i in range(8):
+            racc[i] = psum.tile([P, 512], F32, name="racc%d" % i, tag="bank%d" % i)
+        mm_r(0)
+
+        n_units = len(units)
+        held = []
+        rh_tiles = {}
+        for s in range(2, n_units + 1):
+            if s < n_units:
+                regroup(s)
+            if s == SIG_A:
+                sigmoids(0)
+            if s == SIG_B:
+                sigmoids(1)
+                for a in range(2):
+                    for nb in range(4):
+                        nacc[(a, nb)] = psum.tile([P, 512], F32, name="nacc%d_%d" % (a, nb), tag="bank%d" % (4 * a + nb))
+                for q in held:
+                    mm_n(q)
+                held = []
+            q = s - 1
+            quantise(q)
+            if q < 16:
+                if units[q][1] == 0:
+                    mm_r(q)
+                else:
+                    held.append(q)
+                if q == 15:
+                    for b in sorted(held, key=lambda v: units[v][0]):
+                        mm_r(b)
+                    held = []
+            elif s < SIG_B:
+                held.append(q)
+            else:
+                mm_n(q)
+            if s == SIG_A + 2 or s == SIG_B + 1:
+                half = 0 if s == SIG_A + 2 else 1
+                rh_tiles[half] = gate_h(half)
+            if s == SIG_A + 3 or s == SIG_B + 2:
+                half = 0 if s == SIG_A + 3 else 1
+                quantise_rh(half, rh_tiles[half])
+            if s >= n_units - 1:
+                epilogue(s - (n_units - 1))
+        epilogue(2)
+        epilogue(3)

@@ -18,7 +18,7 @@ B = 256
 H = 2048
 MANUAL = True
 RAW_BUFS = 5
-CV = 480
+CV = 496
 CV_LAST = 192
 SIG_A = 16
 SIG_B = 22
@@ -81,24 +81,24 @@ def tile_grucell_pa_kernel(tc, x, h_prev, W_r, b_r, W_n, b_n, out):
         nc.vector.memset(brt[:], 0.0)
         raw[0] = rawp.tile([P, 8192], BF16, name="raw0", tag="raw")
         xh = rawp.tile([P, 8192], BF16, name="xh", tag="raw")
-        raw0v = raw[0][:].rearrange("p (t n) -> p t n", t=4)
+        raw0v = raw[0][:].rearrange("p (q t n) -> p q t n", q=4, t=4)
         w0 = W_r[0:512, :].rearrange("(p j) n -> p j n", j=4)
         for q in (0, 1):
-            nc.sync.dma_start(out=raw0v[:, :, 512 * q:512 * q + 512], in_=w0[:, :, 512 * q:512 * q + 512])
+            nc.sync.dma_start(out=raw0v[:, q, :, :], in_=w0[:, :, 512 * q:512 * q + 512])
         for a in (0, 1):
             nc.sync.dma_start(out=xh[:, 4096 + 2048 * a:4096 + 2048 * a + 2048], in_=h_prev[P * a:P * a + P, :])
         for a in (0, 1):
             nc.sync.dma_start(out=xh[:, 2048 * a:2048 * a + 2048], in_=x[P * a:P * a + P, :])
         for q in (2, 3):
-            nc.sync.dma_start(out=raw0v[:, :, 512 * q:512 * q + 512], in_=w0[:, :, 512 * q:512 * q + 512])
+            nc.sync.dma_start(out=raw0v[:, q, :, :], in_=w0[:, :, 512 * q:512 * q + 512])
         nc.sync.dma_start(out=brt[0:16, :], in_=b_r.rearrange("(i p) -> i p", p=P))
         for k in range(RAW_BUFS - 2):
             next_load()
 
         units = []
         for c in range(8):
-            units.append((c, 0, 1024, CV, c % 4))
-            units.append((c, 1024, 1024, CV, 4 + c))
+            units.append((c, 0, 1024, CV if c > 0 else 512, c % 4))
+            units.append((c, 1024, 1024, CV if c > 0 else 512, 4 + c))
         for j in range(14):
             units.append((8 + j // 2, 1024 * (j % 2), 1024, CV, j % 12))
         for j in range(4):
@@ -115,14 +115,20 @@ def tile_grucell_pa_kernel(tc, x, h_prev, W_r, b_r, W_n, b_n, out):
             k, n0, w, cv, slot = units[s]
             g = grpp.tile([P, 4096], BF16, name="grp%d" % s, tag="grp", align_bytes=64)
             grouped[s] = g
-            src = raw[k][:].rearrange("p (t n) -> p t n", t=4)
             dst = g[:, 0:4 * w].rearrange("p (n t) -> p n t", t=4)
+            if k == 0:
+                src_v = raw0v[:, n0 // 512, :, :]
+                src_s = raw0v[:, n0 // 512 + 1, :, :]
+            else:
+                src = raw[k][:].rearrange("p (t n) -> p t n", t=4)
+                src_v = src[:, :, n0:n0 + cv]
+                src_s = src[:, :, n0 + cv:n0 + w]
             nc.vector.tensor_copy(
                 out=dst[:, 0:cv, :].rearrange("p (c i) t -> p c t i", i=4),
-                in_=src[:, :, n0:n0 + cv].rearrange("p t (c i) -> p c t i", i=4))
+                in_=src_v.rearrange("p t (c i) -> p c t i", i=4))
             nc.scalar.copy(
                 out=dst[:, cv:w, :].rearrange("p (c i) t -> p c t i", i=4),
-                in_=src[:, :, n0 + cv:n0 + w].rearrange("p t (c i) -> p c t i", i=4))
+                in_=src_s.rearrange("p t (c i) -> p c t i", i=4))
             if last_use[k] == s:
                 next_load()
 

@@ -18,7 +18,7 @@ B = 256
 H = 2048
 MANUAL = True
 RAW_BUFS = 5
-CV = 496
+CV = 560
 CV_LAST = 192
 SIG_A = 16
 SIG_B = 22

@@ -18,7 +18,7 @@ B = 256
 H = 2048
 MANUAL = True
 RAW_BUFS = 5
-CV = 560
+CV = 496
 CV_LAST = 192
 SIG_A = 16
 SIG_B = 22
@@ -69,7 +69,7 @@ def tile_grucell_pa_kernel(tc, x, h_prev, W_r, b_r, W_n, b_n, out):
             else:
                 nc.sync.dma_start(out=t[:].rearrange("p (t n) -> p t n", t=4),
                                   in_=rows.rearrange("(t p) n -> p t n", p=P))
-            if k == 9:
+            if k == 15:
                 nc.sync.dma_start(out=bias_n[:], in_=b_n.partition_broadcast(P))
 
         def next_load():

@@ -17,11 +17,9 @@ P = 128
 B = 256
 H = 2048
 MANUAL = True
-RAW_BUFS = 5
-CV = 496
-CV_LAST = 192
-SIG_A = 16
-SIG_B = 22
+RAW_BUFS = 4
+SIG_A = 9
+SIG_B = 12
 
 
 def tile_grucell_pa_kernel(tc, x, h_prev, W_r, b_r, W_n, b_n, out):
@@ -29,7 +27,7 @@ def tile_grucell_pa_kernel(tc, x, h_prev, W_r, b_r, W_n, b_n, out):
     with ExitStack() as ctx:
         const = ctx.enter_context(tc.tile_pool(name="const", bufs=1))
         rawp = ctx.enter_context(tc.tile_pool(name="rawp", bufs=RAW_BUFS))
-        grpp = ctx.enter_context(tc.tile_pool(name="grpp", bufs=4))
+        grpp = ctx.enter_context(tc.tile_pool(name="grpp", bufs=3))
         codp = ctx.enter_context(tc.tile_pool(name="codp", bufs=1))
         gate = ctx.enter_context(tc.tile_pool(name="gate", bufs=1))
         epi = ctx.enter_context(tc.tile_pool(name="epi", bufs=4))
@@ -95,25 +93,35 @@ def tile_grucell_pa_kernel(tc, x, h_prev, W_r, b_r, W_n, b_n, out):
         for k in range(RAW_BUFS - 2):
             next_load()
 
-        units = []
-        for c in range(8):
-            units.append((c, 0, 1024, CV if c > 0 else 512, c % 4))
-            units.append((c, 1024, 1024, CV if c > 0 else 512, 4 + c))
-        for j in range(14):
-            units.append((8 + j // 2, 1024 * (j % 2), 1024, CV, j % 12))
+        units = [(0, 0, 1024), (0, 1024, 1024)]
+        for k in range(1, 15):
+            units.append((k, 0, 2048))
         for j in range(4):
-            units.append((15, 512 * j, 512, CV_LAST, 2 + j))
+            units.append((15, 512 * j, 512))
         last_use = {}
         for s, u in enumerate(units):
             last_use[u[0]] = s
+        pieces = []
+        pieces_of = {}
+        for s, u in enumerate(units):
+            pieces_of[s] = []
+            for n0 in range(u[1], u[1] + u[2], 1024):
+                q = len(pieces)
+                if q < 16:
+                    slot = (q // 2) % 4 if q % 2 == 0 else 4 + q // 2
+                else:
+                    slot = (q - 16) % 12
+                pieces_of[s].append(q)
+                pieces.append((s, u[0], n0, min(1024, u[2]), slot))
 
         grouped = {}
         codes = {}
         planes = {}
 
         def regroup(s):
-            k, n0, w, cv, slot = units[s]
-            g = grpp.tile([P, 4096], BF16, name="grp%d" % s, tag="grp", align_bytes=64)
+            k, n0, w = units[s]
+            cv = w // 2
+            g = grpp.tile([P, 8192], BF16, name="grp%d" % s, tag="grp", align_bytes=64)
             grouped[s] = g
             dst = g[:, 0:4 * w].rearrange("p (n t) -> p n t", t=4)
             if k == 0:
@@ -132,18 +140,19 @@ def tile_grucell_pa_kernel(tc, x, h_prev, W_r, b_r, W_n, b_n, out):
             if last_use[k] == s:
                 next_load()
 
-        def quantise(s):
-            k, n0, w, cv, slot = units[s]
-            cw = codp.tile([P, 1024], U32, name="cw%d" % s, tag="cw%d" % slot, align_bytes=64)
-            cs = codp.tile([P, 1024], U8, name="cs%d" % s, tag="cs%d" % slot, align_bytes=64)
-            codes[s] = cw
-            planes[s] = cs
-            nc.vector.quantize_mx(out=cw[:, 0:w].bitcast(FP8X4), scales=cs[:, 0:w], in_=grouped[s][:, 0:4 * w])
+        def quantise(q):
+            s, k, n0, w, slot = pieces[q]
+            cw = codp.tile([P, 1024], U32, name="cw%d" % q, tag="cw%d" % slot, align_bytes=64)
+            cs = codp.tile([P, 1024], U8, name="cs%d" % q, tag="cs%d" % slot, align_bytes=64)
+            codes[q] = cw
+            planes[q] = cs
+            g0 = 4 * (n0 - units[s][1])
+            nc.vector.quantize_mx(out=cw[:, 0:w].bitcast(FP8X4), scales=cs[:, 0:w], in_=grouped[s][:, g0:g0 + 4 * w])
 
         racc = {}
 
         def mm_r(s):
-            k, n0, w, cv, slot = units[s]
+            unit, k, n0, w, slot = pieces[s]
             half = n0 // 1024
             nm = "x" if k < 4 else "h"
             a0 = 256 * (k % 4)
@@ -159,7 +168,7 @@ def tile_grucell_pa_kernel(tc, x, h_prev, W_r, b_r, W_n, b_n, out):
         nacc = {}
 
         def mm_n(s):
-            k, n0, w, cv, slot = units[s]
+            unit, k, n0, w, slot = pieces[s]
             c = k - 8
             nm = "x" if c < 4 else "rh"
             for j in range(w // 512):
@@ -234,12 +243,12 @@ def tile_grucell_pa_kernel(tc, x, h_prev, W_r, b_r, W_n, b_n, out):
                            in_=hts[g][:].rearrange("p t b -> p b t"))
         regroup(1)
         nc.vector.quantize_mx(out=act_codes["h"][:].bitcast(FP8X4), scales=act_planes["h"][:], in_=hg[:])
-        xg = grpp.tile([P, 4096], BF16, name="xg", tag="grp", align_bytes=64)
-        xgw = xg[:].bitcast(F32)
+        xg = grpp.tile([P, 8192], BF16, name="xg", tag="grp", align_bytes=64)
+        xgw = xg[:, 0:4096].bitcast(F32)
         for g in range(4):
             nc.vector.tensor_copy(out=xgw[:, 512 * g:512 * g + 512].rearrange("p (b u) -> p b u", u=2),
                                   in_=xts[g][:].rearrange("p u b -> p b u"))
-        nc.vector.quantize_mx(out=act_codes["x"][:].bitcast(FP8X4), scales=act_planes["x"][:], in_=xg[:])
+        nc.vector.quantize_mx(out=act_codes["x"][:].bitcast(FP8X4), scales=act_planes["x"][:], in_=xg[:, 0:4096])
         brp = psum.tile([P, P], BF16, name="brp", tag="bank0")
         nc.tensor.transpose(brp[:], brt[:], ident_bf[:])
         nc.vector.tensor_copy(out=br[:], in_=brp[:, 0:16])
@@ -253,8 +262,6 @@ def tile_grucell_pa_kernel(tc, x, h_prev, W_r, b_r, W_n, b_n, out):
         for s in range(2, n_units + 1):
             if s < n_units:
                 regroup(s)
-            if s == SIG_A:
-                sigmoids(0)
             if s == SIG_B:
                 sigmoids(1)
                 for a in range(2):
@@ -263,26 +270,28 @@ def tile_grucell_pa_kernel(tc, x, h_prev, W_r, b_r, W_n, b_n, out):
                 for q in held:
                     mm_n(q)
                 held = []
-            q = s - 1
-            quantise(q)
-            if q < 16:
-                if units[q][1] == 0:
-                    mm_r(q)
-                else:
+            for q in pieces_of[s - 1]:
+                quantise(q)
+                if q < 16:
+                    if q % 2 == 0:
+                        mm_r(q)
+                    else:
+                        held.append(q)
+                    if q == 14:
+                        sigmoids(0)
+                    if q == 15:
+                        for b in held:
+                            mm_r(b)
+                        held = []
+                elif s < SIG_B:
                     held.append(q)
-                if q == 15:
-                    for b in sorted(held, key=lambda v: units[v][0]):
-                        mm_r(b)
-                    held = []
-            elif s < SIG_B:
-                held.append(q)
-            else:
-                mm_n(q)
-            if s == SIG_A + 2 or s == SIG_B + 1:
-                half = 0 if s == SIG_A + 2 else 1
+                else:
+                    mm_n(q)
+            if s == SIG_A + 1 or s == SIG_B + 1:
+                half = 0 if s == SIG_A + 1 else 1
                 rh_tiles[half] = gate_h(half)
-            if s == SIG_A + 3 or s == SIG_B + 2:
-                half = 0 if s == SIG_A + 3 else 1
+            if s == SIG_A + 2 or s == SIG_B + 2:
+                half = 0 if s == SIG_A + 2 else 1
                 quantise_rh(half, rh_tiles[half])
             if s >= n_units - 1:
                 epilogue(s - (n_units - 1))

@@ -39,6 +39,7 @@ def tile_grucell_pa_kernel(tc, x, h_prev, W_r, b_r, W_n, b_n, out):
         make_identity(nc, ident_f[:])
         brt = const.tile([P, P], BF16, name="brt")
         br = const.tile([P, 16], F32, name="br")
+        warm = const.tile([P, 2], F32, name="warm")
         bias_n = const.tile([P, H], BF16, name="bias_n")
         hg = const.tile([P, 4096], BF16, name="hg", align_bytes=64)
         act_codes = {}
@@ -77,6 +78,8 @@ def tile_grucell_pa_kernel(tc, x, h_prev, W_r, b_r, W_n, b_n, out):
                 state["next_load"] = k + 1
 
         nc.vector.memset(brt[:], 0.0)
+        nc.vector.memset(warm[:, 0:1], 0.0)
+        nc.scalar.activation(out=warm[:, 1:2], in_=warm[:, 0:1], func=ACT.Sigmoid)
         raw[0] = rawp.tile([P, 8192], BF16, name="raw0", tag="raw")
         xh = rawp.tile([P, 8192], BF16, name="xh", tag="raw")
         raw0v = raw[0][:].rearrange("p (q t n) -> p q t n", q=4, t=4)

@@ -197,11 +197,13 @@ def tile_grucell_pa_kernel(tc, x, h_prev, W_r, b_r, W_n, b_n, out):
 
         def gate_h(half):
             rhg = gate.tile([P, 2048], BF16, name="rhg%d" % half, tag="rhg", align_bytes=64)
-            nc.vector.tensor_tensor(
-                out=rhg[:].rearrange("p (g b t) -> p g b t", g=2, t=4),
-                in0=r_sb[half][:].rearrange("p (g t) b -> p g b t", g=2),
-                in1=hg[:, 2048 * half:2048 * half + 2048].rearrange("p (g b t) -> p g b t", g=2, t=4),
-                op=ALU.mult)
+            for g in range(2):
+                h0 = 2048 * half + 1024 * g
+                nc.vector.tensor_tensor(
+                    out=rhg[:, 1024 * g:1024 * g + 1024].rearrange("p (c i t) -> p c t i", i=4, t=4),
+                    in0=r_sb[half][:, 4 * g:4 * g + 4, :].rearrange("p t (c i) -> p c t i", i=4),
+                    in1=hg[:, h0:h0 + 1024].rearrange("p (c i t) -> p c t i", i=4, t=4),
+                    op=ALU.mult)
             return rhg
 
         def quantise_rh(half, rhg):

@@ -18,6 +18,8 @@ B = 256
 H = 2048
 MANUAL = True
 RAW_BUFS = 4
+R_V = 1088
+N_V = 960
 SIG_A = 9
 SIG_B = 12
 
@@ -124,6 +126,8 @@ def tile_grucell_pa_kernel(tc, x, h_prev, W_r, b_r, W_n, b_n, out):
         def regroup(s):
             k, n0, w = units[s]
             cv = w // 2
+            if w == 2048:
+                cv = R_V if k < 8 else N_V
             g = grpp.tile([P, 8192], BF16, name="grp%d" % s, tag="grp", align_bytes=64)
             grouped[s] = g
             dst = g[:, 0:4 * w].rearrange("p (n t) -> p n t", t=4)

@@ -18,7 +18,7 @@ B = 256
 H = 2048
 MANUAL = True
 RAW_BUFS = 4
-R_V = 1088
+R_V = 1024
 N_V = 960
 SIG_A = 9
 SIG_B = 12
@@ -193,21 +193,19 @@ def tile_grucell_pa_kernel(tc, x, h_prev, W_r, b_r, W_n, b_n, out):
         r_sb = {}
 
         def sigmoids(half):
-            r = gate.tile([P, 8, 256], F32, name="r_sb%d" % half, tag="r_sb")
+            r = gate.tile([P, 4, 2, 256], F32, name="r_sb%d" % half, tag="r_sb")
             r_sb[half] = r
             for i in range(8):
-                nc.scalar.activation(out=r[:, i, :], in_=racc[i][:, 256 * half:256 * half + 256],
+                nc.scalar.activation(out=r[:, i % 4, i // 4, :], in_=racc[i][:, 256 * half:256 * half + 256],
                                      func=ACT.Sigmoid, bias=br[:, 8 * half + i:8 * half + i + 1], scale=1.0)
 
         def gate_h(half):
             rhg = gate.tile([P, 2048], BF16, name="rhg%d" % half, tag="rhg", align_bytes=64)
-            for g in range(2):
-                h0 = 2048 * half + 1024 * g
-                nc.vector.tensor_tensor(
-                    out=rhg[:, 1024 * g:1024 * g + 1024].rearrange("p (c i t) -> p c t i", i=4, t=4),
-                    in0=r_sb[half][:, 4 * g:4 * g + 4, :].rearrange("p t (c i) -> p c t i", i=4),
-                    in1=hg[:, h0:h0 + 1024].rearrange("p (c i t) -> p c t i", i=4, t=4),
-                    op=ALU.mult)
+            nc.vector.tensor_tensor(
+                out=rhg[:].rearrange("p (c i t) -> p c t i", i=4, t=4),
+                in0=r_sb[half][:].rearrange("p t g b -> p t (g b)").rearrange("p t (c i) -> p c t i", i=4),
+                in1=hg[:, 2048 * half:2048 * half + 2048].rearrange("p (c i t) -> p c t i", i=4, t=4),
+                op=ALU.mult)
             return rhg
 
         def quantise_rh(half, rhg):

@@ -29,10 +29,9 @@ def tile_grucell_pa_kernel(tc, x, h_prev, W_r, b_r, W_n, b_n, out):
     with ExitStack() as ctx:
         const = ctx.enter_context(tc.tile_pool(name="const", bufs=1))
         rawp = ctx.enter_context(tc.tile_pool(name="rawp", bufs=RAW_BUFS))
-        grpp = ctx.enter_context(tc.tile_pool(name="grpp", bufs=3))
+        grpp = ctx.enter_context(tc.tile_pool(name="grpp", bufs=4))
         codp = ctx.enter_context(tc.tile_pool(name="codp", bufs=1))
         gate = ctx.enter_context(tc.tile_pool(name="gate", bufs=1))
-        epi = ctx.enter_context(tc.tile_pool(name="epi", bufs=4))
         psum = ctx.enter_context(tc.psum_pool(name="psum", bufs=1))
 
         ident_bf = const.tile([P, P], BF16, name="ident_bf")
@@ -212,14 +211,20 @@ def tile_grucell_pa_kernel(tc, x, h_prev, W_r, b_r, W_n, b_n, out):
             nc.vector.quantize_mx(out=act_codes["rh"][:, 512 * half:512 * half + 512].bitcast(FP8X4),
                                   scales=act_planes["rh"][:, 512 * half:512 * half + 512], in_=rhg[:])
 
+        epi = {}
+
         def epilogue(nb):
+            if not epi:
+                epi["pre"] = rawp.tile([P, 4096], F32, name="pre_all", tag="raw")
+                epi["res"] = rawp.tile([P, 4096], F32, name="res_all", tag="raw")
             for a in range(2):
-                pre = epi.tile([P, 512], F32, name="pre%d_%d" % (nb, a), tag="pre")
-                nc.vector.tensor_tensor(out=pre[:], in0=nacc[(a, nb)][:], in1=bias_n[:, 512 * nb:512 * nb + 512],
+                e0 = 512 * (2 * nb + a)
+                pre = epi["pre"][:, e0:e0 + 512]
+                res = epi["res"][:, e0:e0 + 512]
+                nc.vector.tensor_tensor(out=pre, in0=nacc[(a, nb)][:], in1=bias_n[:, 512 * nb:512 * nb + 512],
                                         op=ALU.add)
-                res = epi.tile([P, 512], F32, name="res%d_%d" % (nb, a), tag="res")
-                nc.scalar.activation(out=res[:], in_=pre[:], func=ACT.Tanh)
-                nc.sync.dma_start(out=out[P * a:P * a + P, 512 * nb:512 * nb + 512], in_=res[:])
+                nc.scalar.activation(out=res, in_=pre, func=ACT.Tanh)
+                nc.sync.dma_start(out=out[P * a:P * a + P, 512 * nb:512 * nb + 512], in_=res)
 
         def transposes():
             hts = []

from contextlib import ExitStack

import concourse.mybir as mybir
from concourse.masks import make_identity

FLOPS = 2 * 256 * 2048 * 2048 * 4

BF16 = mybir.dt.bfloat16
F32 = mybir.dt.float32
U32 = mybir.dt.uint32
U8 = mybir.dt.uint8
FP8X4 = mybir.dt.float8_e4m3fn_x4
ACT = mybir.ActivationFunctionType
ALU = mybir.AluOpType

P = 128
B = 256
H = 2048
MANUAL = True
RAW_BUFS = 4
R_V = 1024
N_V = 960
SIG_A = 9
SIG_B = 12


def tile_grucell_pa_kernel(tc, x, h_prev, W_r, b_r, W_n, b_n, out):
    nc = tc.nc
    with ExitStack() as ctx:
        const = ctx.enter_context(tc.tile_pool(name="const", bufs=1))
        rawp = ctx.enter_context(tc.tile_pool(name="rawp", bufs=RAW_BUFS))
        grpp = ctx.enter_context(tc.tile_pool(name="grpp", bufs=4))
        codp = ctx.enter_context(tc.tile_pool(name="codp", bufs=1))
        gate = ctx.enter_context(tc.tile_pool(name="gate", bufs=1))
        psum = ctx.enter_context(tc.psum_pool(name="psum", bufs=1))

        ident_bf = const.tile([P, P], BF16, name="ident_bf")
        ident_f = const.tile([P, P], F32, name="ident_f")
        make_identity(nc, ident_bf[:])
        make_identity(nc, ident_f[:])
        brt = const.tile([P, P], BF16, name="brt")
        br = const.tile([P, 16], F32, name="br")
        warm = const.tile([P, 2], F32, name="warm")
        bias_n = const.tile([P, H], BF16, name="bias_n")
        hg = const.tile([P, 4096], BF16, name="hg", align_bytes=64)
        act_codes = {}
        act_planes = {}
        for nm in ("x", "h", "rh"):
            act_codes[nm] = const.tile([P, 1024], U32, name="codes_" + nm, align_bytes=64)
            act_planes[nm] = const.tile([P, 1024], U8, name="plane_" + nm, align_bytes=64)

        if MANUAL:
            ctx.enter_context(tc.manual_schedule())

        raw = {}
        state = {"next_load": 1}

        def chunk_rows(k):
            w = W_r if k < 8 else W_n
            c = k % 8
            return w[512 * c:512 * c + 512, :], c

        def emit_load(k):
            t = rawp.tile([P, 8192], BF16, name="raw%d" % k, tag="raw")
            raw[k] = t
            rows, c = chunk_rows(k)
            if c < 4:
                nc.sync.dma_start(out=t[:], in_=rows.rearrange("(p j) n -> p (j n)", j=4))
            else:
                nc.sync.dma_start(out=t[:].rearrange("p (t n) -> p t n", t=4),
                                  in_=rows.rearrange("(t p) n -> p t n", p=P))
            if k == 15:
                nc.sync.dma_start(out=bias_n[:], in_=b_n.partition_broadcast(P))

        def next_load():
            k = state["next_load"]
            if k < 16:
                emit_load(k)
                state["next_load"] = k + 1

        nc.vector.memset(brt[:], 0.0)
        nc.vector.memset(warm[:, 0:1], 0.0)
        nc.scalar.activation(out=warm[:, 1:2], in_=warm[:, 0:1], func=ACT.Sigmoid)
        raw[0] = rawp.tile([P, 8192], BF16, name="raw0", tag="raw")
        xh = rawp.tile([P, 8192], BF16, name="xh", tag="raw")
        raw0v = raw[0][:].rearrange("p (q t n) -> p q t n", q=4, t=4)
        w0 = W_r[0:512, :].rearrange("(p j) n -> p j n", j=4)
        for q in (0, 1):
            nc.sync.dma_start(out=raw0v[:, q, :, :], in_=w0[:, :, 512 * q:512 * q + 512])
        for a in (0, 1):
            nc.sync.dma_start(out=xh[:, 4096 + 2048 * a:4096 + 2048 * a + 2048], in_=h_prev[P * a:P * a + P, :])
        for a in (0, 1):
            nc.sync.dma_start(out=xh[:, 2048 * a:2048 * a + 2048], in_=x[P * a:P * a + P, :])
        for q in (2, 3):
            nc.sync.dma_start(out=raw0v[:, q, :, :], in_=w0[:, :, 512 * q:512 * q + 512])
        nc.sync.dma_start(out=brt[0:16, :], in_=b_r.rearrange("(i p) -> i p", p=P))
        for k in range(RAW_BUFS - 2):
            next_load()

        units = [(0, 0, 1024), (0, 1024, 1024)]
        for k in range(1, 15):
            units.append((k, 0, 2048))
        for j in range(4):
            units.append((15, 512 * j, 512))
        last_use = {}
        for s, u in enumerate(units):
            last_use[u[0]] = s
        pieces = []
        pieces_of = {}
        for s, u in enumerate(units):
            pieces_of[s] = []
            for n0 in range(u[1], u[1] + u[2], 1024):
                q = len(pieces)
                if q < 16:
                    slot = (q // 2) % 4 if q % 2 == 0 else 4 + q // 2
                else:
                    slot = (q - 16) % 12
                pieces_of[s].append(q)
                pieces.append((s, u[0], n0, min(1024, u[2]), slot))

        grouped = {}
        codes = {}
        planes = {}

        def regroup(s):
            k, n0, w = units[s]
            cv = w // 2
            if w == 2048:
                cv = R_V if k < 8 else N_V
            g = grpp.tile([P, 8192], BF16, name="grp%d" % s, tag="grp", align_bytes=64)
            grouped[s] = g
            dst = g[:, 0:4 * w].rearrange("p (n t) -> p n t", t=4)
            if k == 0:
                src_v = raw0v[:, n0 // 512, :, :]
                src_s = raw0v[:, n0 // 512 + 1, :, :]
            else:
                src = raw[k][:].rearrange("p (t n) -> p t n", t=4)
                src_v = src[:, :, n0:n0 + cv]
                src_s = src[:, :, n0 + cv:n0 + w]
            nc.vector.tensor_copy(
                out=dst[:, 0:cv, :].rearrange("p (c i) t -> p c t i", i=4),
                in_=src_v.rearrange("p t (c i) -> p c t i", i=4))
            nc.scalar.copy(
                out=dst[:, cv:w, :].rearrange("p (c i) t -> p c t i", i=4),
                in_=src_s.rearrange("p t (c i) -> p c t i", i=4))
            if last_use[k] == s:
                next_load()

        def quantise(q):
            s, k, n0, w, slot = pieces[q]
            cw = codp.tile([P, 1024], U32, name="cw%d" % q, tag="cw%d" % slot, align_bytes=64)
            cs = codp.tile([P, 1024], U8, name="cs%d" % q, tag="cs%d" % slot, align_bytes=64)
            codes[q] = cw
            planes[q] = cs
            g0 = 4 * (n0 - units[s][1])
            nc.vector.quantize_mx(out=cw[:, 0:w].bitcast(FP8X4), scales=cs[:, 0:w], in_=grouped[s][:, g0:g0 + 4 * w])

        racc = {}

        def mm_r(s):
            unit, k, n0, w, slot = pieces[s]
            half = n0 // 1024
            nm = "x" if k < 4 else "h"
            a0 = 256 * (k % 4)
            for i in range(8):
                nc.tensor.matmul_mx(
                    out=racc[i][:, 256 * half:256 * half + 256],
                    lhsT=codes[s][:, P * i:P * i + P].bitcast(FP8X4),
                    lhsT_scale=planes[s][:, P * i:P * i + P],
                    rhs=act_codes[nm][:, a0:a0 + 256].bitcast(FP8X4),
                    rhs_scale=act_planes[nm][:, a0:a0 + 256],
                    start=(k == 0), stop=(k == 7))

        nacc = {}

        def mm_n(s):
            unit, k, n0, w, slot = pieces[s]
            c = k - 8
            nm = "x" if c < 4 else "rh"
            for j in range(w // 512):
                nb = n0 // 512 + j
                for a in range(2):
                    a0 = 256 * (c % 4) + P * a
                    nc.tensor.matmul_mx(
                        out=nacc[(a, nb)][:],
                        lhsT=act_codes[nm][:, a0:a0 + P].bitcast(FP8X4),
                        lhsT_scale=act_planes[nm][:, a0:a0 + P],
                        rhs=codes[s][:, 512 * j:512 * j + 512].bitcast(FP8X4),
                        rhs_scale=planes[s][:, 512 * j:512 * j + 512],
                        start=(c == 0), stop=(c == 7))

        r_sb = {}

        def sigmoids(half):
            r = gate.tile([P, 4, 2, 256], F32, name="r_sb%d" % half, tag="r_sb")
            r_sb[half] = r
            for i in range(8):
                nc.scalar.activation(out=r[:, i % 4, i // 4, :], in_=racc[i][:, 256 * half:256 * half + 256],
                                     func=ACT.Sigmoid, bias=br[:, 8 * half + i:8 * half + i + 1], scale=1.0)

        def gate_h(half):
            rhg = gate.tile([P, 2048], BF16, name="rhg%d" % half, tag="rhg", align_bytes=64)
            nc.vector.tensor_tensor(
                out=rhg[:].rearrange("p (c i t) -> p c t i", i=4, t=4),
                in0=r_sb[half][:].rearrange("p t g b -> p t (g b)").rearrange("p t (c i) -> p c t i", i=4),
                in1=hg[:, 2048 * half:2048 * half + 2048].rearrange("p (c i t) -> p c t i", i=4, t=4),
                op=ALU.mult)
            return rhg

        def quantise_rh(half, rhg):
            nc.vector.quantize_mx(out=act_codes["rh"][:, 512 * half:512 * half + 512].bitcast(FP8X4),
                                  scales=act_planes["rh"][:, 512 * half:512 * half + 512], in_=rhg[:])

        epi = {}

        def epilogue(nb):
            if not epi:
                epi["pre"] = rawp.tile([P, 4096], F32, name="pre_all", tag="raw")
                epi["res"] = rawp.tile([P, 4096], F32, name="res_all", tag="raw")
            for a in range(2):
                e0 = 512 * (2 * nb + a)
                pre = epi["pre"][:, e0:e0 + 512]
                res = epi["res"][:, e0:e0 + 512]
                nc.vector.tensor_tensor(out=pre, in0=nacc[(a, nb)][:], in1=bias_n[:, 512 * nb:512 * nb + 512],
                                        op=ALU.add)
                nc.scalar.activation(out=res, in_=pre, func=ACT.Tanh)
                nc.sync.dma_start(out=out[P * a:P * a + P, 512 * nb:512 * nb + 512], in_=res)

        def transposes():
            hts = []
            for g in range(4):
                ht = psum.tile([P, 4, 256], BF16, name="ht%d" % g, tag="bank%d" % g)
                hts.append(ht)
                for t in range(4):
                    for a in range(2):
                        c0 = 4096 + 2048 * a + 512 * g + P * t
                        nc.tensor.transpose(ht[:, t, P * a:P * a + P], xh[:, c0:c0 + P], ident_bf[:])
            xw = xh[:, 0:4096].bitcast(F32)
            xts = []
            for g in range(4):
                xt = psum.tile([P, 2, 256], F32, name="xt%d" % g, tag="bank%d" % (4 + g))
                xts.append(xt)
                for u in range(2):
                    for a in range(2):
                        c0 = 1024 * a + 256 * g + u
                        nc.tensor.transpose(xt[:, u, P * a:P * a + P], xw[:, c0:c0 + 255:2], ident_f[:])
            return hts, xts

        regroup(0)
        hts, xts = transposes()
        next_load()
        quantise(0)
        for g in range(4):
            nc.scalar.copy(out=hg[:, 1024 * g:1024 * g + 1024].rearrange("p (b t) -> p b t", t=4),
                           in_=hts[g][:].rearrange("p t b -> p b t"))
        regroup(1)
        nc.vector.quantize_mx(out=act_codes["h"][:].bitcast(FP8X4), scales=act_planes["h"][:], in_=hg[:])
        xg = grpp.tile([P, 8192], BF16, name="xg", tag="grp", align_bytes=64)
        xgw = xg[:, 0:4096].bitcast(F32)
        for g in range(4):
            nc.vector.tensor_copy(out=xgw[:, 512 * g:512 * g + 512].rearrange("p (b u) -> p b u", u=2),
                                  in_=xts[g][:].rearrange("p u b -> p b u"))
        nc.vector.quantize_mx(out=act_codes["x"][:].bitcast(FP8X4), scales=act_planes["x"][:], in_=xg[:, 0:4096])
        brp = psum.tile([P, P], BF16, name="brp", tag="bank0")
        nc.tensor.transpose(brp[:], brt[:], ident_bf[:])
        nc.vector.tensor_copy(out=br[:], in_=brp[:, 0:16])
        for i in range(8):
            racc[i] = psum.tile([P, 512], F32, name="racc%d" % i, tag="bank%d" % i)
        mm_r(0)

        n_units = len(units)
        held = []
        rh_tiles = {}
        for s in range(2, n_units + 1):
            if s < n_units:
                regroup(s)
            if s == SIG_B:
                sigmoids(1)
                for a in range(2):
                    for nb in range(4):
                        nacc[(a, nb)] = psum.tile([P, 512], F32, name="nacc%d_%d" % (a, nb), tag="bank%d" % (4 * a + nb))
                for q in held:
                    mm_n(q)
                held = []
            for q in pieces_of[s - 1]:
                quantise(q)
                if q < 16:
                    if q % 2 == 0:
                        mm_r(q)
                    else:
                        held.append(q)
                    if q == 14:
                        sigmoids(0)
                    if q == 15:
                        for b in held:
                            mm_r(b)
                        held = []
                elif s < SIG_B:
                    held.append(q)
                else:
                    mm_n(q)
            if s == SIG_A + 1 or s == SIG_B + 1:
                half = 0 if s == SIG_A + 1 else 1
                rh_tiles[half] = gate_h(half)
            if s == SIG_A + 2 or s == SIG_B + 2:
                half = 0 if s == SIG_A + 2 else 1
                quantise_rh(half, rh_tiles[half])
            if s >= n_units - 1:
                epilogue(s - (n_units - 1))
        epilogue(2)
        epilogue(3)
